import numpy as np
import ml_dtypes


def mxq(x, axis, fmt="e4m3"):
    dtype, down = {"e4m3": (ml_dtypes.float8_e4m3fn, 7), "e5m2": (ml_dtypes.float8_e5m2, 14)}[fmt]
    v = np.moveaxis(np.asarray(x, np.float32).astype(ml_dtypes.bfloat16).astype(np.float64), axis, -1)
    blocks = v.reshape(v.shape[:-1] + (-1, 32))
    amax = np.abs(blocks).max(-1, keepdims=True)
    byte = np.maximum(np.where(amax > 0, np.frexp(amax)[1] - 1 + 127, 0) - down, 1)
    scale = np.exp2(byte - 127.0)
    codes = (blocks / scale).astype(np.float32).astype(dtype).astype(np.float64)
    return np.moveaxis((codes * scale).reshape(v.shape), -1, axis)


WIDE = False


def mx_kscale(k):
    if not WIDE:
        return np.ones(k)
    levels = np.array([20, -20, 10, -10, 0])
    a = np.random.permutation(np.resize(levels, k // 512 * 4)).reshape(k // 512, 4)
    idx = np.arange(k)
    return np.exp2(a[idx // 512, idx % 128 // 32])


BF16 = ml_dtypes.bfloat16


def bf(x):
    return np.asarray(x, np.float32).astype(BF16)


def f64(x):
    return np.asarray(x).astype(np.float64)


B, HH, WW, C, NH, KD, WS, SS = 1, 128, 128, 512, 8, 16, 8, 4
GH, GW, T, F = HH // WS, WW // WS, WS * WS, NH * KD
N = B * GH * GW


def merge_windows(p):
    last = p.shape[-1]
    m = p.reshape(B, GH, GW, WS, WS, last).swapaxes(2, 3).reshape(B, HH, WW, last)
    return np.roll(m, shift=(SS, SS), axis=(1, 2))


def split_windows(g):
    last = g.shape[-1]
    m = np.roll(g, shift=(-SS, -SS), axis=(1, 2))
    return m.reshape(B, GH, WS, GW, WS, last).swapaxes(2, 3).reshape(N * T, last)


def setup_inputs():
    s = mx_kscale(N * T)
    s_win = s.reshape(N, T, 1, 1)
    s_img = merge_windows(s.reshape(N * T, 1))
    attn_ctx = np.random.standard_normal((N, T, NH, KD)) * 0.4 * s_win
    x = np.random.standard_normal((B, HH, WW, C))
    wo = np.random.standard_normal((NH, KD, C)) * 2.0 / np.sqrt(F)
    bo = np.random.standard_normal(C) * 0.3
    g = np.random.standard_normal((B, HH, WW, C)) * np.exp2(np.random.randint(-12, 1, (B, HH, WW, 1))) / s_img
    return {"attn_ctx": bf(attn_ctx), "x": bf(x), "wo": bf(wo), "bo": bf(bo), "grad_out": bf(g)}


def reference(attn_ctx, x, wo, bo, grad_out):
    o = f64(attn_ctx).reshape(N * T, F)
    gw = split_windows(f64(grad_out))
    d = mxq(o, 0, "e4m3").T @ mxq(gw, 0, "e5m2")
    return d.reshape(NH, KD, C)

@@ -1,0 +1,122 @@
+from contextlib import ExitStack
+
+import concourse.mybir as mybir
+
+BF16 = mybir.dt.bfloat16
+F32 = mybir.dt.float32
+U32 = mybir.dt.uint32
+U8 = mybir.dt.uint8
+E4M3X4 = mybir.dt.float8_e4m3fn_x4
+E5M2X4 = mybir.dt.float8_e5m2_x4
+
+P = 128
+PACK = 4
+GRID = 16
+FEATURES = 128
+CHANNELS = 512
+PASSES = 2 * GRID
+TOKENS = PASSES * P * PACK
+
+FLOPS = 2 * TOKENS * FEATURES * CHANNELS
+BYTES = 2 * TOKENS * (FEATURES + CHANNELS) + 4 * FEATURES * CHANNELS
+
+SCALAR_CHANNELS = 320
+STAGE_BUFS = 4
+
+
+def regrouped(dst, src):
+    return (
+        dst.rearrange("p (c i) t -> p c t i", i=4),
+        src.rearrange("p t (c i) -> p c t i", i=4),
+    )
+
+
+def tile_windowattentionblock_pb_k_kernel(tc, attn_ctx, x, wo, bo, grad_out, out):
+    nc = tc.nc
+    with ExitStack() as ctx:
+        ctx.enter_context(tc.manual_schedule())
+        resident = ctx.enter_context(tc.tile_pool(name="resident", bufs=1))
+        loads = ctx.enter_context(tc.tile_pool(name="loads", bufs=PASSES))
+        stage = ctx.enter_context(tc.tile_pool(name="stage", bufs=STAGE_BUFS))
+        psum = ctx.enter_context(tc.psum_pool(name="psum", bufs=1))
+
+        a_view = attn_ctx.rearrange(
+            "(gi gj) (th r j) h d -> th gj gi r (j h d)", gj=GRID, th=2, r=8
+        )
+        g_view = grad_out.rearrange(
+            "b (q rh s) (v j) c -> b rh v q s (j c)", rh=2, s=4, j=PACK
+        )
+
+        a_raw = resident.tile([P, PASSES, PACK * FEATURES], BF16)
+        g_raws = []
+        for th in range(2):
+            for gj in range(GRID):
+                i = th * GRID + gj
+                if th == 0:
+                    nc.sync.dma_start(out=a_raw[:, i, :], in_=a_view[0, gj])
+                else:
+                    nc.sync.dma_start(out=a_raw[8:P, i, :], in_=a_view[1, gj, 0 : GRID - 1])
+                g_raw = loads.tile([P, PACK * CHANNELS], BF16)
+                g_raws.append(g_raw)
+                for h in range(2):
+                    v = (2 * gj + 1 + h) % (2 * GRID)
+                    nc.sync.dma_start(out=g_raw[h:P:2, :], in_=g_view[0, 1 - th, v])
+            if th == 0:
+                nc.sync.dma_start(
+                    out=a_raw[0:8, GRID:PASSES, :],
+                    in_=a_view[1, :, GRID - 1].rearrange("g r e -> r g e"),
+                )
+
+        acc = psum.tile([FEATURES, CHANNELS], F32)
+        grouped = {}
+
+        def regroup(i):
+            a_grouped = stage.tile([P, FEATURES, PACK], BF16, align_bytes=64)
+            g_grouped = stage.tile([P, CHANNELS, PACK], BF16, align_bytes=64)
+            grouped[i] = (a_grouped, g_grouped)
+            a_src = a_raw[:, i, :].rearrange("p (t c) -> p t c", t=PACK)
+            g_src = g_raws[i][:].rearrange("p (t c) -> p t c", t=PACK)
+            dst, src = regrouped(g_grouped[:, 0:SCALAR_CHANNELS, :], g_src[:, :, 0:SCALAR_CHANNELS])
+            nc.scalar.copy(out=dst, in_=src)
+            dst, src = regrouped(a_grouped[:], a_src)
+            nc.vector.tensor_copy(out=dst, in_=src)
+            dst, src = regrouped(
+                g_grouped[:, SCALAR_CHANNELS:CHANNELS, :], g_src[:, :, SCALAR_CHANNELS:CHANNELS]
+            )
+            nc.vector.tensor_copy(out=dst, in_=src)
+
+        def quantise_and_multiply(i):
+            a_grouped, g_grouped = grouped[i]
+            a_codes = stage.tile([P, FEATURES], U32, align_bytes=64)
+            a_scales = stage.tile([P, FEATURES], U8, align_bytes=64)
+            g_codes = stage.tile([P, CHANNELS], U32, align_bytes=64)
+            g_scales = stage.tile([P, CHANNELS], U8, align_bytes=64)
+            nc.vector.quantize_mx(
+                out=a_codes[:].bitcast(E4M3X4),
+                scales=a_scales[:],
+                in_=a_grouped[:].rearrange("p c t -> p (c t)"),
+            )
+            nc.vector.quantize_mx(
+                out=g_codes[:].bitcast(E5M2X4),
+                scales=g_scales[:],
+                in_=g_grouped[:].rearrange("p c t -> p (c t)"),
+            )
+            nc.tensor.matmul_mx(
+                out=acc[:],
+                lhsT=a_codes[:].bitcast(E4M3X4),
+                lhsT_scale=a_scales[:],
+                rhs=g_codes[:].bitcast(E5M2X4),
+                rhs_scale=g_scales[:],
+                start=(i == 0),
+                stop=(i == PASSES - 1),
+            )
+
+        regroup(0)
+        for i in range(1, PASSES):
+            regroup(i)
+            quantise_and_multiply(i - 1)
+        quantise_and_multiply(PASSES - 1)
+
+        result = resident.tile([FEATURES, CHANNELS], F32)
+        nc.scalar.copy(out=result[:], in_=acc[:])
+        nc.sync.dma_start(out=out.rearrange("h d c -> (h d) c"), in_=result[:])

@@ -21,6 +21,7 @@ FLOPS = 2 * TOKENS * FEATURES * CHANNELS
 BYTES = 2 * TOKENS * (FEATURES + CHANNELS) + 4 * FEATURES * CHANNELS
 
 SCALAR_CHANNELS = 320
+CHUNK = 4
 STAGE_BUFS = 4
 
 
@@ -36,36 +37,46 @@ def tile_windowattentionblock_pb_k_kernel(tc, attn_ctx, x, wo, bo, grad_out, out
     with ExitStack() as ctx:
         ctx.enter_context(tc.manual_schedule())
         resident = ctx.enter_context(tc.tile_pool(name="resident", bufs=1))
-        loads = ctx.enter_context(tc.tile_pool(name="loads", bufs=PASSES))
+        loads = ctx.enter_context(tc.tile_pool(name="loads", bufs=PASSES // CHUNK))
         stage = ctx.enter_context(tc.tile_pool(name="stage", bufs=STAGE_BUFS))
         psum = ctx.enter_context(tc.psum_pool(name="psum", bufs=1))
 
-        a_view = attn_ctx.rearrange(
-            "(gi gj) (th r j) h d -> th gj gi r (j h d)", gj=GRID, th=2, r=8
-        )
-        g_view = grad_out.rearrange(
-            "b (q rh s) (v j) c -> b rh v q s (j c)", rh=2, s=4, j=PACK
+        a_win = attn_ctx.rearrange("(gi gj) (r j) h d -> gi r gj (j h d)", gj=GRID, r=16)
+        g_halves = grad_out.rearrange(
+            "b (rh r) (g two j) c -> b rh two r g (j c)", rh=2, two=2, j=PACK
         )
 
         a_raw = resident.tile([P, PASSES, PACK * FEATURES], BF16)
         g_raws = []
-        for th in range(2):
-            for gj in range(GRID):
-                i = th * GRID + gj
-                if th == 0:
-                    nc.sync.dma_start(out=a_raw[:, i, :], in_=a_view[0, gj])
-                else:
-                    nc.sync.dma_start(out=a_raw[8:P, i, :], in_=a_view[1, gj, 0 : GRID - 1])
-                g_raw = loads.tile([P, PACK * CHANNELS], BF16)
-                g_raws.append(g_raw)
-                for h in range(2):
-                    v = (2 * gj + 1 + h) % (2 * GRID)
-                    nc.sync.dma_start(out=g_raw[h:P:2, :], in_=g_view[0, 1 - th, v])
-            if th == 0:
+
+        def load_attn(rh):
+            slots = slice(rh * GRID, (rh + 1) * GRID)
+            nc.sync.dma_start(out=a_raw[0:8, slots, :], in_=a_win[(8 * rh - 1) % GRID, 8:16])
+            for a in range(7):
                 nc.sync.dma_start(
-                    out=a_raw[0:8, GRID:PASSES, :],
-                    in_=a_view[1, :, GRID - 1].rearrange("g r e -> r g e"),
+                    out=a_raw[8 + 16 * a : 24 + 16 * a, slots, :], in_=a_win[8 * rh + a]
                 )
+            nc.sync.dma_start(out=a_raw[120:P, slots, :], in_=a_win[8 * rh + 7, 0:8])
+
+        def load_grad(rh, chunk):
+            g_raw = loads.tile([P, CHUNK, PACK * CHANNELS], BF16)
+            g_raws.append(g_raw)
+            gj = chunk * CHUNK
+            nc.sync.dma_start(out=g_raw[0:P:2, :, :], in_=g_halves[0, rh, 1, :, gj : gj + CHUNK, :])
+            if gj + CHUNK < GRID:
+                nc.sync.dma_start(
+                    out=g_raw[1:P:2, :, :], in_=g_halves[0, rh, 0, :, gj + 1 : gj + 1 + CHUNK, :]
+                )
+            else:
+                nc.sync.dma_start(
+                    out=g_raw[1:P:2, 0 : CHUNK - 1, :], in_=g_halves[0, rh, 0, :, gj + 1 : GRID, :]
+                )
+                nc.sync.dma_start(out=g_raw[1:P:2, CHUNK - 1, :], in_=g_halves[0, rh, 0, :, 0, :])
+
+        for rh in range(2):
+            load_attn(rh)
+            for chunk in range(GRID // CHUNK):
+                load_grad(rh, chunk)
 
         acc = psum.tile([FEATURES, CHANNELS], F32)
         grouped = {}
@@ -75,7 +86,7 @@ def tile_windowattentionblock_pb_k_kernel(tc, attn_ctx, x, wo, bo, grad_out, out
             g_grouped = stage.tile([P, CHANNELS, PACK], BF16, align_bytes=64)
             grouped[i] = (a_grouped, g_grouped)
             a_src = a_raw[:, i, :].rearrange("p (t c) -> p t c", t=PACK)
-            g_src = g_raws[i][:].rearrange("p (t c) -> p t c", t=PACK)
+            g_src = g_raws[i // CHUNK][:, i % CHUNK, :].rearrange("p (t c) -> p t c", t=PACK)
             dst, src = regrouped(g_grouped[:, 0:SCALAR_CHANNELS, :], g_src[:, :, 0:SCALAR_CHANNELS])
             nc.scalar.copy(out=dst, in_=src)
             dst, src = regrouped(a_grouped[:], a_src)

@@ -20,8 +20,7 @@ TOKENS = PASSES * P * PACK
 FLOPS = 2 * TOKENS * FEATURES * CHANNELS
 BYTES = 2 * TOKENS * (FEATURES + CHANNELS) + 4 * FEATURES * CHANNELS
 
-SCALAR_CHANNELS = 320
-CHUNK = 4
+SCALAR_CHANNELS = 192
 STAGE_BUFS = 4
 
 
@@ -37,46 +36,36 @@ def tile_windowattentionblock_pb_k_kernel(tc, attn_ctx, x, wo, bo, grad_out, out
     with ExitStack() as ctx:
         ctx.enter_context(tc.manual_schedule())
         resident = ctx.enter_context(tc.tile_pool(name="resident", bufs=1))
-        loads = ctx.enter_context(tc.tile_pool(name="loads", bufs=PASSES // CHUNK))
+        loads = ctx.enter_context(tc.tile_pool(name="loads", bufs=PASSES))
         stage = ctx.enter_context(tc.tile_pool(name="stage", bufs=STAGE_BUFS))
         psum = ctx.enter_context(tc.psum_pool(name="psum", bufs=1))
 
-        a_win = attn_ctx.rearrange("(gi gj) (r j) h d -> gi r gj (j h d)", gj=GRID, r=16)
-        g_halves = grad_out.rearrange(
-            "b (rh r) (g two j) c -> b rh two r g (j c)", rh=2, two=2, j=PACK
+        a_view = attn_ctx.rearrange(
+            "(gi gj) (th r j) h d -> th gj gi r (j h d)", gj=GRID, th=2, r=8
+        )
+        g_view = grad_out.rearrange(
+            "b (q rh s) (v j) c -> b rh v q s (j c)", rh=2, s=4, j=PACK
         )
 
         a_raw = resident.tile([P, PASSES, PACK * FEATURES], BF16)
         g_raws = []
-
-        def load_attn(rh):
-            slots = slice(rh * GRID, (rh + 1) * GRID)
-            nc.sync.dma_start(out=a_raw[0:8, slots, :], in_=a_win[(8 * rh - 1) % GRID, 8:16])
-            for a in range(7):
+        for th in range(2):
+            for gj in range(GRID):
+                i = th * GRID + gj
+                if th == 0:
+                    nc.sync.dma_start(out=a_raw[:, i, :], in_=a_view[0, gj])
+                else:
+                    nc.sync.dma_start(out=a_raw[8:P, i, :], in_=a_view[1, gj, 0 : GRID - 1])
+                g_raw = loads.tile([P, PACK * CHANNELS], BF16)
+                g_raws.append(g_raw)
+                for h in range(2):
+                    v = (2 * gj + 1 + h) % (2 * GRID)
+                    nc.sync.dma_start(out=g_raw[h:P:2, :], in_=g_view[0, 1 - th, v])
+            if th == 0:
                 nc.sync.dma_start(
-                    out=a_raw[8 + 16 * a : 24 + 16 * a, slots, :], in_=a_win[8 * rh + a]
+                    out=a_raw[0:8, GRID:PASSES, :],
+                    in_=a_view[1, :, GRID - 1].rearrange("g r e -> r g e"),
                 )
-            nc.sync.dma_start(out=a_raw[120:P, slots, :], in_=a_win[8 * rh + 7, 0:8])
-
-        def load_grad(rh, chunk):
-            g_raw = loads.tile([P, CHUNK, PACK * CHANNELS], BF16)
-            g_raws.append(g_raw)
-            gj = chunk * CHUNK
-            nc.sync.dma_start(out=g_raw[0:P:2, :, :], in_=g_halves[0, rh, 1, :, gj : gj + CHUNK, :])
-            if gj + CHUNK < GRID:
-                nc.sync.dma_start(
-                    out=g_raw[1:P:2, :, :], in_=g_halves[0, rh, 0, :, gj + 1 : gj + 1 + CHUNK, :]
-                )
-            else:
-                nc.sync.dma_start(
-                    out=g_raw[1:P:2, 0 : CHUNK - 1, :], in_=g_halves[0, rh, 0, :, gj + 1 : GRID, :]
-                )
-                nc.sync.dma_start(out=g_raw[1:P:2, CHUNK - 1, :], in_=g_halves[0, rh, 0, :, 0, :])
-
-        for rh in range(2):
-            load_attn(rh)
-            for chunk in range(GRID // CHUNK):
-                load_grad(rh, chunk)
 
         acc = psum.tile([FEATURES, CHANNELS], F32)
         grouped = {}
@@ -86,7 +75,7 @@ def tile_windowattentionblock_pb_k_kernel(tc, attn_ctx, x, wo, bo, grad_out, out
             g_grouped = stage.tile([P, CHANNELS, PACK], BF16, align_bytes=64)
             grouped[i] = (a_grouped, g_grouped)
             a_src = a_raw[:, i, :].rearrange("p (t c) -> p t c", t=PACK)
-            g_src = g_raws[i // CHUNK][:, i % CHUNK, :].rearrange("p (t c) -> p t c", t=PACK)
+            g_src = g_raws[i][:].rearrange("p (t c) -> p t c", t=PACK)
             dst, src = regrouped(g_grouped[:, 0:SCALAR_CHANNELS, :], g_src[:, :, 0:SCALAR_CHANNELS])
             nc.scalar.copy(out=dst, in_=src)
             dst, src = regrouped(a_grouped[:], a_src)

@@ -20,7 +20,7 @@ TOKENS = PASSES * P * PACK
 FLOPS = 2 * TOKENS * FEATURES * CHANNELS
 BYTES = 2 * TOKENS * (FEATURES + CHANNELS) + 4 * FEATURES * CHANNELS
 
-SCALAR_CHANNELS = 192
+SCALAR_CHANNELS = 320
 STAGE_BUFS = 4
 
 
@@ -40,32 +40,40 @@ def tile_windowattentionblock_pb_k_kernel(tc, attn_ctx, x, wo, bo, grad_out, out
         stage = ctx.enter_context(tc.tile_pool(name="stage", bufs=STAGE_BUFS))
         psum = ctx.enter_context(tc.psum_pool(name="psum", bufs=1))
 
-        a_view = attn_ctx.rearrange(
-            "(gi gj) (th r j) h d -> th gj gi r (j h d)", gj=GRID, th=2, r=8
+        a_win = attn_ctx.rearrange("(gi gj) (r j) h d -> gi r gj (j h d)", gj=GRID, r=16)
+        g_halves = grad_out.rearrange(
+            "b (rh r) (g two j) c -> b rh two r g (j c)", rh=2, two=2, j=PACK
         )
-        g_view = grad_out.rearrange(
-            "b (q rh s) (v j) c -> b rh v q s (j c)", rh=2, s=4, j=PACK
-        )
+
+        g_rows = grad_out.rearrange("b (rh r) w c -> b rh r (w c)", rh=2)
 
         a_raw = resident.tile([P, PASSES, PACK * FEATURES], BF16)
         g_raws = []
-        for th in range(2):
-            for gj in range(GRID):
-                i = th * GRID + gj
-                if th == 0:
-                    nc.sync.dma_start(out=a_raw[:, i, :], in_=a_view[0, gj])
-                else:
-                    nc.sync.dma_start(out=a_raw[8:P, i, :], in_=a_view[1, gj, 0 : GRID - 1])
-                g_raw = loads.tile([P, PACK * CHANNELS], BF16)
-                g_raws.append(g_raw)
-                for h in range(2):
-                    v = (2 * gj + 1 + h) % (2 * GRID)
-                    nc.sync.dma_start(out=g_raw[h:P:2, :], in_=g_view[0, 1 - th, v])
-            if th == 0:
+
+        def load_attn(rh):
+            slots = slice(rh * GRID, (rh + 1) * GRID)
+            nc.sync.dma_start(out=a_raw[0:8, slots, :], in_=a_win[(8 * rh - 1) % GRID, 8:16])
+            for a in range(7):
                 nc.sync.dma_start(
-                    out=a_raw[0:8, GRID:PASSES, :],
-                    in_=a_view[1, :, GRID - 1].rearrange("g r e -> r g e"),
+                    out=a_raw[8 + 16 * a : 24 + 16 * a, slots, :], in_=a_win[8 * rh + a]
                 )
+            nc.sync.dma_start(out=a_raw[120:P, slots, :], in_=a_win[8 * rh + 7, 0:8])
+
+        def load_grad(rh, gj):
+            g_raw = loads.tile([P, PACK * CHANNELS], BF16)
+            g_raws.append(g_raw)
+            if gj < GRID - 1:
+                first = (8 * gj + 4) * CHANNELS
+                run = g_rows[0, rh, :, first : first + 8 * CHANNELS]
+                nc.sync.dma_start(out=g_raw[:], in_=run.rearrange("r (h e) -> r h e", h=2))
+            else:
+                nc.sync.dma_start(out=g_raw[0:P:2, :], in_=g_halves[0, rh, 1, :, gj, :])
+                nc.sync.dma_start(out=g_raw[1:P:2, :], in_=g_halves[0, rh, 0, :, 0, :])
+
+        for rh in range(2):
+            load_attn(rh)
+            for gj in range(GRID):
+                load_grad(rh, gj)
 
         acc = psum.tile([FEATURES, CHANNELS], F32)
         grouped = {}

@@ -40,40 +40,23 @@ def tile_windowattentionblock_pb_k_kernel(tc, attn_ctx, x, wo, bo, grad_out, out
         stage = ctx.enter_context(tc.tile_pool(name="stage", bufs=STAGE_BUFS))
         psum = ctx.enter_context(tc.psum_pool(name="psum", bufs=1))
 
-        a_win = attn_ctx.rearrange("(gi gj) (r j) h d -> gi r gj (j h d)", gj=GRID, r=16)
-        g_halves = grad_out.rearrange(
-            "b (rh r) (g two j) c -> b rh two r g (j c)", rh=2, two=2, j=PACK
+        a_view = attn_ctx.rearrange(
+            "(gi gj) (th r j) h d -> gi th gj r (j h d)", gj=GRID, th=2, r=8
         )
-
-        g_rows = grad_out.rearrange("b (rh r) w c -> b rh r (w c)", rh=2)
+        g_view = grad_out.rearrange(
+            "b (rb s) (g two j) c -> b rb two g s (j c)", s=4, two=2, j=PACK
+        )
 
         a_raw = resident.tile([P, PASSES, PACK * FEATURES], BF16)
         g_raws = []
-
-        def load_attn(rh):
-            slots = slice(rh * GRID, (rh + 1) * GRID)
-            nc.sync.dma_start(out=a_raw[0:8, slots, :], in_=a_win[(8 * rh - 1) % GRID, 8:16])
-            for a in range(7):
-                nc.sync.dma_start(
-                    out=a_raw[8 + 16 * a : 24 + 16 * a, slots, :], in_=a_win[8 * rh + a]
-                )
-            nc.sync.dma_start(out=a_raw[120:P, slots, :], in_=a_win[8 * rh + 7, 0:8])
-
-        def load_grad(rh, gj):
+        for rb in range(PASSES):
+            window_half = (rb - 1) % PASSES
+            nc.sync.dma_start(out=a_raw[:, rb, :], in_=a_view[window_half // 2, window_half % 2])
             g_raw = loads.tile([P, PACK * CHANNELS], BF16)
             g_raws.append(g_raw)
-            if gj < GRID - 1:
-                first = (8 * gj + 4) * CHANNELS
-                run = g_rows[0, rh, :, first : first + 8 * CHANNELS]
-                nc.sync.dma_start(out=g_raw[:], in_=run.rearrange("r (h e) -> r h e", h=2))
-            else:
-                nc.sync.dma_start(out=g_raw[0:P:2, :], in_=g_halves[0, rh, 1, :, gj, :])
-                nc.sync.dma_start(out=g_raw[1:P:2, :], in_=g_halves[0, rh, 0, :, 0, :])
-
-        for rh in range(2):
-            load_attn(rh)
-            for gj in range(GRID):
-                load_grad(rh, gj)
+            nc.sync.dma_start(out=g_raw[0:P:2, :], in_=g_view[0, rb, 1])
+            nc.sync.dma_start(out=g_raw[1 : P - 8 : 2, :], in_=g_view[0, rb, 0, 1:GRID])
+            nc.sync.dma_start(out=g_raw[P - 7 : P : 2, :], in_=g_view[0, rb, 0, 0])
 
         acc = psum.tile([FEATURES, CHANNELS], F32)
         grouped = {}

@@ -51,7 +51,7 @@ def tile_windowattentionblock_pb_k_kernel(tc, attn_ctx, x, wo, bo, grad_out, out
         g_raws = []
         for rb in range(PASSES):
             window_half = (rb - 1) % PASSES
-            nc.sync.dma_start(out=a_raw[:, rb, :], in_=a_view[window_half // 2, window_half % 2])
+            nc.gpsimd.dma_start(out=a_raw[:, rb, :], in_=a_view[window_half // 2, window_half % 2])
             g_raw = loads.tile([P, PACK * CHANNELS], BF16)
             g_raws.append(g_raw)
             nc.sync.dma_start(out=g_raw[0:P:2, :], in_=g_view[0, rb, 1])

@@ -41,22 +41,33 @@ def tile_windowattentionblock_pb_k_kernel(tc, attn_ctx, x, wo, bo, grad_out, out
         psum = ctx.enter_context(tc.psum_pool(name="psum", bufs=1))
 
         a_view = attn_ctx.rearrange(
-            "(gi gj) (th r j) h d -> gi th gj r (j h d)", gj=GRID, th=2, r=8
+            "(gi gj) (th r j) h d -> th gj gi r (j h d)", gj=GRID, th=2, r=8
         )
         g_view = grad_out.rearrange(
-            "b (rb s) (g two j) c -> b rb two g s (j c)", s=4, two=2, j=PACK
+            "b (q rh s) (v j) c -> b rh v q s (j c)", rh=2, s=4, j=PACK
         )
 
         a_raw = resident.tile([P, PASSES, PACK * FEATURES], BF16)
         g_raws = []
-        for rb in range(PASSES):
-            window_half = (rb - 1) % PASSES
-            nc.gpsimd.dma_start(out=a_raw[:, rb, :], in_=a_view[window_half // 2, window_half % 2])
-            g_raw = loads.tile([P, PACK * CHANNELS], BF16)
-            g_raws.append(g_raw)
-            nc.sync.dma_start(out=g_raw[0:P:2, :], in_=g_view[0, rb, 1])
-            nc.sync.dma_start(out=g_raw[1 : P - 8 : 2, :], in_=g_view[0, rb, 0, 1:GRID])
-            nc.sync.dma_start(out=g_raw[P - 7 : P : 2, :], in_=g_view[0, rb, 0, 0])
+        for th in range(2):
+            for gj in range(GRID):
+                i = th * GRID + gj
+                if th == 0:
+                    nc.sync.dma_start(out=a_raw[:, i, :], in_=a_view[0, gj])
+                else:
+                    nc.sync.dma_start(out=a_raw[8:P, i, :], in_=a_view[1, gj, 0 : GRID - 1])
+                g_raw = loads.tile([P, PACK * CHANNELS], BF16)
+                g_raws.append(g_raw)
+                for h in range(2):
+                    v = (2 * gj + 1 + h) % (2 * GRID)
+                    rows = g_view[0, 1 - th, v].rearrange("q (s1 s0) e -> s0 q s1 e", s0=2)
+                    for s0 in range(2):
+                        nc.sync.dma_start(out=g_raw[2 * s0 + h : P : 4, :], in_=rows[s0])
+            if th == 0:
+                nc.sync.dma_start(
+                    out=a_raw[0:8, GRID:PASSES, :],
+                    in_=a_view[1, :, GRID - 1].rearrange("g r e -> r g e"),
+                )
 
         acc = psum.tile([FEATURES, CHANNELS], F32)
         grouped = {}

@@ -58,10 +58,10 @@ def tile_windowattentionblock_pb_k_kernel(tc, attn_ctx, x, wo, bo, grad_out, out
                     nc.sync.dma_start(out=a_raw[8:P, i, :], in_=a_view[1, gj, 0 : GRID - 1])
                 g_raw = loads.tile([P, PACK * CHANNELS], BF16)
                 g_raws.append(g_raw)
-                for h in range(2):
-                    v = (2 * gj + 1 + h) % (2 * GRID)
-                    rows = g_view[0, 1 - th, v].rearrange("q (s1 s0) e -> s0 q s1 e", s0=2)
-                    for s0 in range(2):
+                for s0 in range(2):
+                    for h in range(2):
+                        v = (2 * gj + 1 + h) % (2 * GRID)
+                        rows = g_view[0, 1 - th, v].rearrange("q (s1 s0) e -> s0 q s1 e", s0=2)
                         nc.sync.dma_start(out=g_raw[2 * s0 + h : P : 4, :], in_=rows[s0])
             if th == 0:
                 nc.sync.dma_start(

from contextlib import ExitStack

import concourse.mybir as mybir

BF16 = mybir.dt.bfloat16
F32 = mybir.dt.float32
U32 = mybir.dt.uint32
U8 = mybir.dt.uint8
E4M3X4 = mybir.dt.float8_e4m3fn_x4
E5M2X4 = mybir.dt.float8_e5m2_x4

P = 128
PACK = 4
GRID = 16
FEATURES = 128
CHANNELS = 512
PASSES = 2 * GRID
TOKENS = PASSES * P * PACK

FLOPS = 2 * TOKENS * FEATURES * CHANNELS
BYTES = 2 * TOKENS * (FEATURES + CHANNELS) + 4 * FEATURES * CHANNELS

SCALAR_CHANNELS = 320
STAGE_BUFS = 4


def regrouped(dst, src):
    return (
        dst.rearrange("p (c i) t -> p c t i", i=4),
        src.rearrange("p t (c i) -> p c t i", i=4),
    )


def tile_windowattentionblock_pb_k_kernel(tc, attn_ctx, x, wo, bo, grad_out, out):
    nc = tc.nc
    with ExitStack() as ctx:
        ctx.enter_context(tc.manual_schedule())
        resident = ctx.enter_context(tc.tile_pool(name="resident", bufs=1))
        loads = ctx.enter_context(tc.tile_pool(name="loads", bufs=PASSES))
        stage = ctx.enter_context(tc.tile_pool(name="stage", bufs=STAGE_BUFS))
        psum = ctx.enter_context(tc.psum_pool(name="psum", bufs=1))

        a_view = attn_ctx.rearrange(
            "(gi gj) (th r j) h d -> th gj gi r (j h d)", gj=GRID, th=2, r=8
        )
        g_view = grad_out.rearrange(
            "b (q rh s) (v j) c -> b rh v q s (j c)", rh=2, s=4, j=PACK
        )

        a_raw = resident.tile([P, PASSES, PACK * FEATURES], BF16)
        g_raws = []
        for th in range(2):
            for gj in range(GRID):
                i = th * GRID + gj
                if th == 0:
                    nc.sync.dma_start(out=a_raw[:, i, :], in_=a_view[0, gj])
                else:
                    nc.sync.dma_start(out=a_raw[8:P, i, :], in_=a_view[1, gj, 0 : GRID - 1])
                g_raw = loads.tile([P, PACK * CHANNELS], BF16)
                g_raws.append(g_raw)
                for s0 in range(2):
                    for h in range(2):
                        v = (2 * gj + 1 + h) % (2 * GRID)
                        rows = g_view[0, 1 - th, v].rearrange("q (s1 s0) e -> s0 q s1 e", s0=2)
                        nc.sync.dma_start(out=g_raw[2 * s0 + h : P : 4, :], in_=rows[s0])
            if th == 0:
                nc.sync.dma_start(
                    out=a_raw[0:8, GRID:PASSES, :],
                    in_=a_view[1, :, GRID - 1].rearrange("g r e -> r g e"),
                )

        acc = psum.tile([FEATURES, CHANNELS], F32)
        grouped = {}

        def regroup(i):
            a_grouped = stage.tile([P, FEATURES, PACK], BF16, align_bytes=64)
            g_grouped = stage.tile([P, CHANNELS, PACK], BF16, align_bytes=64)
            grouped[i] = (a_grouped, g_grouped)
            a_src = a_raw[:, i, :].rearrange("p (t c) -> p t c", t=PACK)
            g_src = g_raws[i][:].rearrange("p (t c) -> p t c", t=PACK)
            dst, src = regrouped(g_grouped[:, 0:SCALAR_CHANNELS, :], g_src[:, :, 0:SCALAR_CHANNELS])
            nc.scalar.copy(out=dst, in_=src)
            dst, src = regrouped(a_grouped[:], a_src)
            nc.vector.tensor_copy(out=dst, in_=src)
            dst, src = regrouped(
                g_grouped[:, SCALAR_CHANNELS:CHANNELS, :], g_src[:, :, SCALAR_CHANNELS:CHANNELS]
            )
            nc.vector.tensor_copy(out=dst, in_=src)

        def quantise_and_multiply(i):
            a_grouped, g_grouped = grouped[i]
            a_codes = stage.tile([P, FEATURES], U32, align_bytes=64)
            a_scales = stage.tile([P, FEATURES], U8, align_bytes=64)
            g_codes = stage.tile([P, CHANNELS], U32, align_bytes=64)
            g_scales = stage.tile([P, CHANNELS], U8, align_bytes=64)
            nc.vector.quantize_mx(
                out=a_codes[:].bitcast(E4M3X4),
                scales=a_scales[:],
                in_=a_grouped[:].rearrange("p c t -> p (c t)"),
            )
            nc.vector.quantize_mx(
                out=g_codes[:].bitcast(E5M2X4),
                scales=g_scales[:],
                in_=g_grouped[:].rearrange("p c t -> p (c t)"),
            )
            nc.tensor.matmul_mx(
                out=acc[:],
                lhsT=a_codes[:].bitcast(E4M3X4),
                lhsT_scale=a_scales[:],
                rhs=g_codes[:].bitcast(E5M2X4),
                rhs_scale=g_scales[:],
                start=(i == 0),
                stop=(i == PASSES - 1),
            )

        regroup(0)
        for i in range(1, PASSES):
            regroup(i)
            quantise_and_multiply(i - 1)
        quantise_and_multiply(PASSES - 1)

        result = resident.tile([FEATURES, CHANNELS], F32)
        nc.scalar.copy(out=result[:], in_=acc[:])
        nc.sync.dma_start(out=out.rearrange("h d c -> (h d) c"), in_=result[:])
